import numpy as np
import ml_dtypes


def mxq(x, axis, fmt="e4m3"):
    dtype, down = {"e4m3": (ml_dtypes.float8_e4m3fn, 7), "e5m2": (ml_dtypes.float8_e5m2, 14)}[fmt]
    v = np.moveaxis(np.asarray(x, np.float32).astype(ml_dtypes.bfloat16).astype(np.float64), axis, -1)
    blocks = v.reshape(v.shape[:-1] + (-1, 32))
    amax = np.abs(blocks).max(-1, keepdims=True)
    byte = np.maximum(np.where(amax > 0, np.frexp(amax)[1] - 1 + 127, 0) - down, 1)
    scale = np.exp2(byte - 127.0)
    codes = (blocks / scale).astype(np.float32).astype(dtype).astype(np.float64)
    return np.moveaxis((codes * scale).reshape(v.shape), -1, axis)


WIDE = False


def mx_kscale(k):
    if not WIDE:
        return np.ones(k)
    levels = np.array([30, -30])
    if k % 512:
        return np.exp2(np.random.permutation(np.resize(levels, k // 32))).repeat(32)
    a = np.empty((k // 512, 16))
    for p in range(k // 512):
        a[p, :8] = np.random.permutation(np.resize(levels, 8))
        for g in range(8):
            far = levels[np.abs(levels - a[p, g]) >= 10]
            a[p, g + 8] = far[np.random.randint(len(far))]
    return np.exp2(a.ravel()).repeat(32)


BF16 = ml_dtypes.bfloat16


def bf(x):
    return np.asarray(x, np.float32).astype(BF16)


def f64(x):
    return np.asarray(x).astype(np.float64)


B, D, E = 2, 1024, 1024
S = E // 2


def rope(y):
    n = y.shape[-1]
    inv_freq = 1.0 / (10000.0 ** (np.arange(0.0, n, 2.0) / n))
    freqs = inv_freq * np.arange(y.shape[1], dtype=np.float64)
    sin = np.sin(freqs)[None, :, None]
    cos = np.cos(freqs)[None, :, None]
    y1 = y[..., ::2]
    y2 = y[..., 1::2]
    return np.concatenate([y1 * cos - y2 * sin, y1 * sin + y2 * cos], axis=-1)


def setup_inputs():
    s = mx_kscale(D)
    return {"x": bf(np.random.standard_normal((B, S, D)) * s),
            "Wk": bf(np.random.standard_normal((E, D)) / np.sqrt(D) / s[None, :]),
            "bk": bf(np.random.standard_normal(E) * 0.3),
            "Wq": bf(np.random.standard_normal((E, D)) / np.sqrt(D) / s[None, :]),
            "bq": bf(np.random.standard_normal(E) * 0.3),
            "Wv": bf(np.random.standard_normal((E, D)) / np.sqrt(D) / s[None, :]),
            "bv": bf(np.random.standard_normal(E) * 0.3)}


def reference(x, Wk, bk, Wq, bq, Wv, bv):
    xq = mxq(f64(x), 2, "e5m2")
    K = rope((xq @ mxq(f64(Wk), 1, "e5m2").T) + f64(bk))
    Q = rope((xq @ mxq(f64(Wq), 1, "e5m2").T) + f64(bq))
    V = (xq @ mxq(f64(Wv), 1, "e5m2").T) + f64(bv)
    return (K, Q, V)

@@ -1,0 +1,306 @@
+import math
+from contextlib import ExitStack
+
+import concourse.mybir as mybir
+from concourse.masks import make_identity
+
+B, S, D, E = 2, 512, 1024, 1024
+FLOPS = 2 * B * S * D * 3 * E
+
+F32 = mybir.dt.float32
+BF16 = mybir.dt.bfloat16
+I32 = mybir.dt.int32
+U32 = mybir.dt.uint32
+U8 = mybir.dt.uint8
+MX = mybir.dt.float8_e5m2_x4
+ALU = mybir.AluOpType
+ACT = mybir.ActivationFunctionType
+
+P = 128
+HALF = 512
+MK, MQ, MV = 0, 1, 2
+X_CHUNKS = [(0, 0), (1, 0), (0, 1), (1, 1)]
+
+
+def tile_attention_kernel(tc, x, Wk, bk, Wq, bq, Wv, bv, out_0, out_1, out_2):
+    nc = tc.nc
+    weights = [Wk, Wq, Wv]
+    biases = [bk, bq, bv]
+    outs = [o.rearrange("b (c p j) e -> b c j p e", p=P, j=2) for o in (out_0, out_1, out_2)]
+    x_rows = x.rearrange("b (c p j) d -> b c p j d", p=P, j=2)
+    w_rows = [w.rearrange("(c p j) d -> c p j d", p=P, j=2) for w in weights]
+
+    with ExitStack() as ctx:
+        keep = ctx.enter_context(tc.tile_pool(name="keep", bufs=1))
+        stage = ctx.enter_context(tc.tile_pool(name="stage", bufs=4))
+        ypool = ctx.enter_context(tc.tile_pool(name="ypool", bufs=8))
+        apool = ctx.enter_context(tc.tile_pool(name="apool", bufs=4))
+        tpsum = ctx.enter_context(tc.psum_pool(name="tpsum", bufs=4))
+        mpsum = ctx.enter_context(tc.psum_pool(name="mpsum", bufs=4))
+        ctx.enter_context(tc.manual_schedule())
+
+        brows = keep.tile([P, E], BF16, name="brows")
+        nc.vector.memset(brows[:].bitcast(I32), 0)
+        for m in range(3):
+            nc.scalar.dma_start(out=brows[m:m + 1, :], in_=biases[m].rearrange("(o e) -> o e", o=1))
+
+        raw = {}
+
+        def load(key, src, pieces=1):
+            t = keep.tile([P, 2, D], BF16, name="raw_%s_%d" % key)
+            raw[key] = t
+            w = D // pieces
+            for i in range(pieces):
+                nc.sync.dma_start(out=t[:, :, i * w:(i + 1) * w], in_=src[:, :, i * w:(i + 1) * w])
+
+        def load_w(m, c, pieces=1):
+            load(("w%d" % m, c), w_rows[m][c], pieces)
+
+        def load_x(n):
+            load(("x", n), x_rows[X_CHUNKS[n][0], X_CHUNKS[n][1]])
+
+        load_w(MK, 0, 2)
+        load_w(MK, 1)
+        load_x(0)
+        load_w(MK, 2)
+        load_w(MK, 3)
+        load_x(1)
+        load_w(MQ, 0)
+        load_w(MQ, 1)
+        load_x(2)
+        load_x(3)
+        load_w(MQ, 2)
+        load_w(MQ, 3)
+        for c in range(4):
+            load_w(MV, c)
+
+
+        pos = keep.tile([P, 4], F32, name="pos")
+        base = keep.tile([P, 4], F32, name="base")
+        expo = keep.tile([P, 4], F32, name="expo")
+        invf = keep.tile([P, 4], F32, name="invf")
+        nc.gpsimd.iota(pos[:], pattern=[[256, 2], [1, 2]], base=0, channel_multiplier=2,
+                       allow_small_or_imprecise_dtypes=True)
+        nc.gpsimd.memset(base[:], 10000.0)
+        nc.gpsimd.tensor_scalar(expo[:], pos[:], -2.0 / E, 0.0, op0=ALU.mult, op1=ALU.add)
+        nc.gpsimd.tensor_tensor(invf[:], base[:], expo[:], op=ALU.pow)
+        ident = keep.tile([P, P], F32, name="ident")
+        make_identity(nc, ident[:])
+
+        turns = keep.tile([P, 8], F32, name="turns")
+        whole = keep.tile([P, 8], I32, name="whole")
+        frac = keep.tile([P, 8], F32, name="frac")
+        nfrac = keep.tile([P, 8], F32, name="nfrac")
+        sincos = keep.tile([P, 8], F32, name="sincos")
+        rcos = keep.tile([P, 4], F32, name="rcos")
+        tan = keep.tile([P, 4], F32, name="tan")
+        sel = keep.tile([P, 4], BF16, name="sel")
+        nc.vector.scalar_tensor_tensor(turns[:, 0:4], invf[:], 1.0 / (2.0 * math.pi), pos[:], op0=ALU.mult, op1=ALU.mult)
+        nc.vector.tensor_scalar(turns[:, 4:8], turns[:, 0:4], 0.25, None, op0=ALU.add)
+        nc.vector.tensor_copy(whole[:], turns[:])
+        nc.vector.tensor_tensor(frac[:], turns[:], whole[:], op=ALU.subtract)
+        nc.vector.scalar_tensor_tensor(nfrac[:], frac[:], 0.5, frac[:], op0=ALU.is_gt, op1=ALU.subtract)
+        nc.vector.tensor_copy(sel[:], ident[:, 0:4])
+        nc.scalar.activation(sincos[:], nfrac[:], ACT.Sin, scale=-2.0 * math.pi)
+        nc.vector.reciprocal(rcos[:], sincos[:, 4:8])
+        nc.vector.tensor_tensor(tan[:], sincos[:, 0:4], rcos[:], op=ALU.mult)
+
+        bias_sb = {}
+
+        def spread_bias(m, eng):
+            pb = tpsum.tile([P, E], BF16, name="tb", tag="tb")
+            for j in range(2):
+                cols = brows[:, j * HALF:(j + 1) * HALF] if m == MV else brows[:, j:E:2]
+                nc.tensor.matmul(pb[:, j * HALF:(j + 1) * HALF], lhsT=sel[:, m:m + 1].to_broadcast([P, P]),
+                                 rhs=cols, start=True, stop=True)
+            t = keep.tile([P, E], BF16, name="bias%d" % m)
+            bias_sb[m] = t
+            copy_on(eng, t[:], pb[:])
+
+        def copy_on(eng, out, in_):
+            if eng == "v":
+                nc.vector.tensor_copy(out, in_)
+            else:
+                nc.scalar.copy(out, in_)
+
+        tables = {}
+
+        def table_tile(m, a):
+            if (m, a) not in tables:
+                tables[(m, a)] = keep.tile([P, E], F32, name="cb%d_%d" % (m, a))
+            return tables[(m, a)]
+
+        def table_v(m, a):
+            nc.vector.tensor_scalar(table_tile(m, a)[:], bias_sb[m][:], sincos[:, 4 + a:5 + a], None, op0=ALU.mult)
+
+        def table_s(m, a, j):
+            cols = slice(j * HALF, (j + 1) * HALF)
+            nc.scalar.activation(table_tile(m, a)[:, cols], bias_sb[m][:, cols], ACT.Copy, scale=sincos[:, 4 + a:5 + a])
+
+        staged = {}
+        codes = {}
+        scales = {}
+
+        def transpose_bank(key, g):
+            bank = tpsum.tile([P, 2, 2, P], F32, name="tb", tag="tb")
+            for j in range(2):
+                words = raw[key][:, j, :].bitcast(F32)
+                for u in range(2):
+                    nc.tensor.transpose(bank[:, j, u, :], words[:, 256 * g + u:256 * (g + 1):2], ident[:])
+            return bank
+
+        def stage_tile(unit):
+            if unit not in staged:
+                staged[unit] = stage.tile([P, 4 * HALF], BF16, name="staged", tag="staged", align_bytes=64)
+            return staged[unit][:].bitcast(F32)
+
+        def bank_job(job):
+            if job[0] == "w":
+                m, c, g = job[1:]
+                bank = transpose_bank(("w%d" % m, c), g)
+                dst = stage_tile(("w", m, c // 2, g)).rearrange("p (j c r u) -> p j c r u", j=2, c=2, u=2)[:, :, c % 2, :, :]
+            else:
+                n, g = job[1:]
+                bank = transpose_bank(("x", n), g)
+                dst = stage_tile(("x", n)).rearrange("p (g j r u) -> p g j r u", g=2, j=2, u=2)[:, g, :, :, :]
+            return bank, dst
+
+        def copy_bank(bank_dst, eng):
+            bank, dst = bank_dst
+            copy_on(eng, dst, bank[:].rearrange("p j u r -> p j r u"))
+
+        def quantize(unit):
+            name = "_".join(str(v) for v in unit)
+            codes[unit] = keep.tile([P, HALF], U32, name="codes_" + name, align_bytes=64)
+            scales[unit] = keep.tile([P, HALF], U8, name="scales_" + name, align_bytes=64)
+            nc.vector.quantize_mx(out=codes[unit][:].bitcast(MX), scales=scales[unit][:], in_=staged[unit][:])
+
+        def unit_jobs(unit):
+            if unit[0] == "w":
+                return [("w", unit[1], 2 * unit[2] + c, unit[3]) for c in range(2)]
+            return [("x", unit[1], g) for g in range(2)]
+
+        banks = {}
+        ys = {}
+        scaled = {}
+
+        def multiply(m, n):
+            xu = ("x", n // 2)
+            for h in range(2):
+                bank = mpsum.tile([P, HALF], F32, name="mb", tag="mb")
+                banks[(m, n, h)] = bank
+                for g in range(2):
+                    cols = slice(256 * g + P * (n % 2), 256 * g + P * (n % 2) + P)
+                    wu = ("w", m, h, g)
+                    nc.tensor.matmul_mx(out=bank[:], lhsT=codes[xu][:, cols].bitcast(MX), lhsT_scale=scales[xu][:, cols],
+                                        rhs=codes[wu][:].bitcast(MX), rhs_scale=scales[wu][:],
+                                        start=(g == 0), stop=(g == 1))
+
+        def angle_col(n):
+            return 2 * X_CHUNKS[n // 2][1] + n % 2
+
+        def add_bias(m, n):
+            y = ypool.tile([P, E], F32, name="y", tag="y")
+            ys[(m, n)] = y
+            for h in range(2):
+                bank = banks[(m, n, h)]
+                if m == MV:
+                    cols = slice(h * HALF, (h + 1) * HALF)
+                    nc.vector.tensor_tensor(y[:, cols].rearrange("p (r j) -> p r j", j=2),
+                                            bank[:].rearrange("p (j r) -> p r j", j=2),
+                                            bias_sb[m][:, cols].rearrange("p (r j) -> p r j", j=2), op=ALU.add)
+                else:
+                    a = angle_col(n)
+                    nc.vector.scalar_tensor_tensor(
+                        y[:].rearrange("p (j h r) -> p j h r", j=2, h=2)[:, :, h, :],
+                        bank[:].rearrange("p (j r) -> p j r", j=2),
+                        sincos[:, 4 + a:5 + a],
+                        tables[(m, a)][:].rearrange("p (j h r) -> p j h r", j=2, h=2)[:, :, h, :],
+                        op0=ALU.mult, op1=ALU.add)
+
+        def scale_tan(m, n, both):
+            t = apool.tile([P, E], F32, name="ty", tag="ty")
+            scaled[(m, n)] = t
+            a = angle_col(n)
+            cols = slice(0 if both else HALF, E)
+            nc.scalar.activation(t[:, cols], ys[(m, n)][:, cols], ACT.Copy, scale=tan[:, a:a + 1])
+
+        def rotate_upper_v(m, n):
+            y = ys[(m, n)]
+            a = angle_col(n)
+            nc.vector.scalar_tensor_tensor(y[:, HALF:E], y[:, 0:HALF], tan[:, a:a + 1], y[:, HALF:E], op0=ALU.mult, op1=ALU.add)
+
+        def rotate_g(m, n, both):
+            y = ys[(m, n)]
+            t = scaled[(m, n)]
+            nc.gpsimd.tensor_tensor(y[:, 0:HALF], y[:, 0:HALF], t[:, HALF:E], op=ALU.subtract)
+            if both:
+                nc.gpsimd.tensor_tensor(y[:, HALF:E], y[:, HALF:E], t[:, 0:HALF], op=ALU.add)
+
+        def store(m, n):
+            b, c = X_CHUNKS[n // 2]
+            nc.sync.dma_start(out=outs[m][b, c, n % 2], in_=ys[(m, n)][:])
+
+        spread_bias(MK, "s")
+        copy_bank(bank_job(("w", MK, 0, 0)), "s")
+        copy_bank(bank_job(("w", MK, 0, 1)), "v")
+        spread_bias(MQ, "s")
+        table_v(MK, 0)
+        copy_bank(bank_job(("w", MK, 1, 0)), "s")
+        copy_bank(bank_job(("w", MK, 1, 1)), "s")
+        quantize(("w", MK, 0, 0))
+        spread_bias(MV, "s")
+        copy_bank(bank_job(("x", 0, 0)), "v")
+        quantize(("w", MK, 0, 1))
+        copy_bank(bank_job(("x", 0, 1)), "s")
+        table_v(MK, 1)
+        copy_bank(bank_job(("w", MK, 2, 0)), "s")
+        quantize(("x", 0))
+        copy_bank(bank_job(("w", MK, 2, 1)), "v")
+        copy_bank(bank_job(("w", MK, 3, 0)), "s")
+        copy_bank(bank_job(("w", MK, 3, 1)), "s")
+        quantize(("w", MK, 1, 0))
+        quantize(("w", MK, 1, 1))
+
+        units = [("x", 1), ("w", MQ, 0, 0), ("x", 2), ("w", MQ, 0, 1), ("x", 3), ("w", MQ, 1, 0), ("w", MQ, 1, 1)]
+        units += [("w", MV, h, g) for h in range(2) for g in range(2)]
+        slots = [(MK, n) for n in range(8)] + [(MQ, n) for n in range(4)]
+        for n in range(4):
+            slots += [(MQ, 4 + n), (MV, n)]
+        slots += [(MV, n) for n in range(4, 8)]
+        table_halves = [(m, a, j) for m, a in ((MK, 2), (MK, 3), (MQ, 0), (MQ, 1), (MQ, 2), (MQ, 3)) for j in range(2)]
+        ALL_G_FROM = 12
+
+        def at(seq, i):
+            return seq[i] if 0 <= i < len(seq) else None
+
+        def store_delay(s):
+            if slots[s][0] == MV:
+                return 2
+            return 5 if s >= ALL_G_FROM else 3
+
+        for s in range(len(slots) + 5):
+            unit = at(units, s)
+            if at(table_halves, s):
+                table_s(*table_halves[s])
+            if unit:
+                for job in unit_jobs(unit):
+                    copy_bank(bank_job(job), "s")
+            if at(slots, s):
+                multiply(*slots[s])
+            prev = at(slots, s - 1)
+            if prev:
+                add_bias(*prev)
+                if prev[0] != MV:
+                    scale_tan(*prev, s - 1 >= ALL_G_FROM)
+            if at(units, s - 1):
+                quantize(units[s - 1])
+            prev2 = at(slots, s - 2)
+            if prev2 and prev2[0] != MV and s - 2 < ALL_G_FROM:
+                rotate_upper_v(*prev2)
+                rotate_g(*prev2, False)
+            if prev and prev[0] != MV and s - 1 >= ALL_G_FROM:
+                rotate_g(*prev, True)
+            for r in range(len(slots)):
+                if r + store_delay(r) == s:
+                    store(*slots[r])

@@ -22,6 +22,37 @@ MK, MQ, MV = 0, 1, 2
 X_CHUNKS = [(0, 0), (1, 0), (0, 1), (1, 1)]
 
 
+def LOADS(load_w, load_x):
+    for c in "x2 q0 q1 x3 q2 q3 v0 v1 v2 v3".split():
+        if c[0] == "x":
+            load_x(int(c[1]))
+        else:
+            load_w(MQ if c[0] == "q" else MV, int(c[1]))
+
+
+def PLAN(wq, wv):
+    tiles = [({"k": MK, "q": MQ, "v": MV}[c[0]], int(c[1])) for c in "k0 k1 k2 k3 k4 k5 k6 k7 q0 q1 q2 v0 q3 v1 q4 v2 q5 v3 q6 v4 q7 v5 v6 v7".split()]
+    units = [[("x", int(u[1])) if u[0] == "x" else (wq if u[0] == "q" else wv)[int(u[1])] for u in c.split(",") if u != "-"] for c in "- - x2 q0 x3,q1 q2 q3 v0 v1 v2 v3".split()]
+    return [(units[i] if i < len(units) else [], t) for i, t in enumerate(tiles)]
+
+
+def ONG(m, n):
+    return (m, n) in [(MQ, 2), (MQ, 3), (MQ, 4), (MQ, 5), (MQ, 6), (MQ, 7)]
+
+
+def TAB(s):
+    return min(12, 2 * (s - 3) if s < 7 else s + 1)
+
+
+def DELAY(m, n):
+    return 1 if m == MV else (5 if ONG(m, n) else 3)
+
+
+SPLIT = False
+VCOPY = 0
+OQ = 1
+
+
 def tile_attention_kernel(tc, x, Wk, bk, Wq, bq, Wv, bv, out_0, out_1, out_2):
     nc = tc.nc
     weights = [Wk, Wq, Wv]
@@ -65,57 +96,56 @@ def tile_attention_kernel(tc, x, Wk, bk, Wq, bq, Wv, bv, out_0, out_1, out_2):
         load_w(MK, 2)
         load_w(MK, 3)
         load_x(1)
-        load_w(MQ, 0)
-        load_w(MQ, 1)
-        load_x(2)
-        load_x(3)
-        load_w(MQ, 2)
-        load_w(MQ, 3)
-        for c in range(4):
-            load_w(MV, c)
+        LOADS(load_w, load_x)
 
 
+        ident = keep.tile([P, P], F32, name="ident")
+        sel = keep.tile([P, 4], BF16, name="sel")
         pos = keep.tile([P, 4], F32, name="pos")
         base = keep.tile([P, 4], F32, name="base")
         expo = keep.tile([P, 4], F32, name="expo")
         invf = keep.tile([P, 4], F32, name="invf")
+        nc.vector.memset(base[:], 10000.0)
+        nc.vector.memset(ident[:], 0.0)
         nc.gpsimd.iota(pos[:], pattern=[[256, 2], [1, 2]], base=0, channel_multiplier=2,
                        allow_small_or_imprecise_dtypes=True)
-        nc.gpsimd.memset(base[:], 10000.0)
         nc.gpsimd.tensor_scalar(expo[:], pos[:], -2.0 / E, 0.0, op0=ALU.mult, op1=ALU.add)
         nc.gpsimd.tensor_tensor(invf[:], base[:], expo[:], op=ALU.pow)
-        ident = keep.tile([P, P], F32, name="ident")
-        make_identity(nc, ident[:])
+        make_identity(nc, ident[:], nomemset=True)
 
         turns = keep.tile([P, 8], F32, name="turns")
         whole = keep.tile([P, 8], I32, name="whole")
         frac = keep.tile([P, 8], F32, name="frac")
-        nfrac = keep.tile([P, 8], F32, name="nfrac")
         sincos = keep.tile([P, 8], F32, name="sincos")
         rcos = keep.tile([P, 4], F32, name="rcos")
         tan = keep.tile([P, 4], F32, name="tan")
-        sel = keep.tile([P, 4], BF16, name="sel")
+        ntan = keep.tile([P, 4], F32, name="ntan")
         nc.vector.scalar_tensor_tensor(turns[:, 0:4], invf[:], 1.0 / (2.0 * math.pi), pos[:], op0=ALU.mult, op1=ALU.mult)
         nc.vector.tensor_scalar(turns[:, 4:8], turns[:, 0:4], 0.25, None, op0=ALU.add)
         nc.vector.tensor_copy(whole[:], turns[:])
-        nc.vector.tensor_tensor(frac[:], turns[:], whole[:], op=ALU.subtract)
-        nc.vector.scalar_tensor_tensor(nfrac[:], frac[:], 0.5, frac[:], op0=ALU.is_gt, op1=ALU.subtract)
         nc.vector.tensor_copy(sel[:], ident[:, 0:4])
-        nc.scalar.activation(sincos[:], nfrac[:], ACT.Sin, scale=-2.0 * math.pi)
-        nc.vector.reciprocal(rcos[:], sincos[:, 4:8])
-        nc.vector.tensor_tensor(tan[:], sincos[:, 0:4], rcos[:], op=ALU.mult)
+        nc.vector.tensor_tensor(frac[:], turns[:], whole[:], op=ALU.subtract)
+        nc.scalar.activation(sincos[:], frac[:], ACT.Sin, scale=2.0 * math.pi)
+
+        def tangents():
+            nc.vector.reciprocal(rcos[:], sincos[:, 4:8])
+            nc.vector.tensor_tensor(tan[:], sincos[:, 0:4], rcos[:], op=ALU.mult)
+            nc.vector.scalar_tensor_tensor(ntan[:], sincos[:, 0:4], -1.0, rcos[:], op0=ALU.mult, op1=ALU.mult)
 
         bias_sb = {}
 
-        def spread_bias(m, eng):
-            pb = tpsum.tile([P, E], BF16, name="tb", tag="tb")
-            for j in range(2):
-                cols = brows[:, j * HALF:(j + 1) * HALF] if m == MV else brows[:, j:E:2]
-                nc.tensor.matmul(pb[:, j * HALF:(j + 1) * HALF], lhsT=sel[:, m:m + 1].to_broadcast([P, P]),
-                                 rhs=cols, start=True, stop=True)
-            t = keep.tile([P, E], BF16, name="bias%d" % m)
-            bias_sb[m] = t
-            copy_on(eng, t[:], pb[:])
+        bias_ps = {}
+
+        def spread_bias(m, j):
+            if j == 0:
+                bias_ps[m] = mpsum.tile([P, E], BF16, name="mb", tag="mb")
+            pb = bias_ps[m]
+            cols = brows[:, j * HALF:(j + 1) * HALF] if m == MV else brows[:, j:E:2]
+            nc.tensor.matmul(pb[:, j * HALF:(j + 1) * HALF], lhsT=sel[:, m:m + 1].to_broadcast([P, P]),
+                             rhs=cols, start=True, stop=True)
+            if j == 1:
+                bias_sb[m] = keep.tile([P, E], BF16, name="bias%d" % m)
+                nc.scalar.copy(bias_sb[m][:], pb[:])
 
         def copy_on(eng, out, in_):
             if eng == "v":
@@ -132,6 +162,9 @@ def tile_attention_kernel(tc, x, Wk, bk, Wq, bq, Wv, bv, out_0, out_1, out_2):
 
         def table_v(m, a):
             nc.vector.tensor_scalar(table_tile(m, a)[:], bias_sb[m][:], sincos[:, 4 + a:5 + a], None, op0=ALU.mult)
+
+        def table_g(m, a):
+            nc.gpsimd.tensor_scalar(table_tile(m, a)[:], bias_sb[m][:], sincos[:, 4 + a:5 + a], 0.0, op0=ALU.mult, op1=ALU.add)
 
         def table_s(m, a, j):
             cols = slice(j * HALF, (j + 1) * HALF)
@@ -184,46 +217,47 @@ def tile_attention_kernel(tc, x, Wk, bk, Wq, bq, Wv, bv, out_0, out_1, out_2):
         ys = {}
         scaled = {}
 
-        def multiply(m, n):
+        def multiply(m, n, h):
             xu = ("x", n // 2)
-            for h in range(2):
-                bank = mpsum.tile([P, HALF], F32, name="mb", tag="mb")
-                banks[(m, n, h)] = bank
-                for g in range(2):
-                    cols = slice(256 * g + P * (n % 2), 256 * g + P * (n % 2) + P)
-                    wu = ("w", m, h, g)
-                    nc.tensor.matmul_mx(out=bank[:], lhsT=codes[xu][:, cols].bitcast(MX), lhsT_scale=scales[xu][:, cols],
-                                        rhs=codes[wu][:].bitcast(MX), rhs_scale=scales[wu][:],
-                                        start=(g == 0), stop=(g == 1))
+            bank = mpsum.tile([P, HALF], F32, name="mb", tag="mb")
+            banks[(m, n, h)] = bank
+            for g in range(2):
+                cols = slice(256 * g + P * (n % 2), 256 * g + P * (n % 2) + P)
+                wu = ("w", m, h, g)
+                nc.tensor.matmul_mx(out=bank[:], lhsT=codes[xu][:, cols].bitcast(MX), lhsT_scale=scales[xu][:, cols],
+                                    rhs=codes[wu][:].bitcast(MX), rhs_scale=scales[wu][:],
+                                    start=(g == 0), stop=(g == 1))
 
         def angle_col(n):
             return 2 * X_CHUNKS[n // 2][1] + n % 2
 
-        def add_bias(m, n):
-            y = ypool.tile([P, E], F32, name="y", tag="y")
-            ys[(m, n)] = y
-            for h in range(2):
-                bank = banks[(m, n, h)]
-                if m == MV:
-                    cols = slice(h * HALF, (h + 1) * HALF)
-                    nc.vector.tensor_tensor(y[:, cols].rearrange("p (r j) -> p r j", j=2),
-                                            bank[:].rearrange("p (j r) -> p r j", j=2),
-                                            bias_sb[m][:, cols].rearrange("p (r j) -> p r j", j=2), op=ALU.add)
-                else:
-                    a = angle_col(n)
-                    nc.vector.scalar_tensor_tensor(
-                        y[:].rearrange("p (j h r) -> p j h r", j=2, h=2)[:, :, h, :],
-                        bank[:].rearrange("p (j r) -> p j r", j=2),
-                        sincos[:, 4 + a:5 + a],
-                        tables[(m, a)][:].rearrange("p (j h r) -> p j h r", j=2, h=2)[:, :, h, :],
-                        op0=ALU.mult, op1=ALU.add)
+        def add_bias(m, n, h):
+            if h == 0:
+                ys[(m, n)] = ypool.tile([P, E], F32, name="y", tag="y")
+            y = ys[(m, n)]
+            bank = banks[(m, n, h)]
+            if m == MV:
+                cols = slice(h * HALF, (h + 1) * HALF)
+                nc.vector.tensor_tensor(y[:, cols].rearrange("p (r j) -> p r j", j=2),
+                                        bank[:].rearrange("p (j r) -> p r j", j=2),
+                                        bias_sb[m][:, cols].rearrange("p (r j) -> p r j", j=2), op=ALU.add)
+            else:
+                a = angle_col(n)
+                nc.vector.scalar_tensor_tensor(
+                    y[:].rearrange("p (j h r) -> p j h r", j=2, h=2)[:, :, h, :],
+                    bank[:].rearrange("p (j r) -> p j r", j=2),
+                    sincos[:, 4 + a:5 + a],
+                    tables[(m, a)][:].rearrange("p (j h r) -> p j h r", j=2, h=2)[:, :, h, :],
+                    op0=ALU.mult, op1=ALU.add)
 
         def scale_tan(m, n, both):
             t = apool.tile([P, E], F32, name="ty", tag="ty")
             scaled[(m, n)] = t
             a = angle_col(n)
-            cols = slice(0 if both else HALF, E)
-            nc.scalar.activation(t[:, cols], ys[(m, n)][:, cols], ACT.Copy, scale=tan[:, a:a + 1])
+            y = ys[(m, n)]
+            nc.scalar.activation(t[:, 0:HALF], y[:, HALF:E], ACT.Copy, scale=ntan[:, a:a + 1])
+            if both:
+                nc.scalar.activation(t[:, HALF:E], y[:, 0:HALF], ACT.Copy, scale=tan[:, a:a + 1])
 
         def rotate_upper_v(m, n):
             y = ys[(m, n)]
@@ -232,75 +266,109 @@ def tile_attention_kernel(tc, x, Wk, bk, Wq, bq, Wv, bv, out_0, out_1, out_2):
 
         def rotate_g(m, n, both):
             y = ys[(m, n)]
-            t = scaled[(m, n)]
-            nc.gpsimd.tensor_tensor(y[:, 0:HALF], y[:, 0:HALF], t[:, HALF:E], op=ALU.subtract)
-            if both:
-                nc.gpsimd.tensor_tensor(y[:, HALF:E], y[:, HALF:E], t[:, 0:HALF], op=ALU.add)
+            cols = slice(0, E if both else HALF)
+            nc.gpsimd.tensor_tensor(y[:, cols], y[:, cols], scaled[(m, n)][:, cols], op=ALU.add)
 
-        def store(m, n):
+        def store(m, n, pieces=1):
             b, c = X_CHUNKS[n // 2]
-            nc.sync.dma_start(out=outs[m][b, c, n % 2], in_=ys[(m, n)][:])
+            w = E // pieces
+            for i in range(pieces):
+                nc.sync.dma_start(out=outs[m][b, c, n % 2][:, i * w:(i + 1) * w], in_=ys[(m, n)][:, i * w:(i + 1) * w])
 
-        spread_bias(MK, "s")
         copy_bank(bank_job(("w", MK, 0, 0)), "s")
+        spread_bias(MK, 0)
+        spread_bias(MK, 1)
         copy_bank(bank_job(("w", MK, 0, 1)), "v")
-        spread_bias(MQ, "s")
-        table_v(MK, 0)
         copy_bank(bank_job(("w", MK, 1, 0)), "s")
-        copy_bank(bank_job(("w", MK, 1, 1)), "s")
+        spread_bias(MQ, 0)
+        copy_bank(bank_job(("w", MK, 1, 1)), "v")
         quantize(("w", MK, 0, 0))
-        spread_bias(MV, "s")
-        copy_bank(bank_job(("x", 0, 0)), "v")
+        copy_bank(bank_job(("x", 0, 0)), "s")
+        spread_bias(MQ, 1)
         quantize(("w", MK, 0, 1))
-        copy_bank(bank_job(("x", 0, 1)), "s")
-        table_v(MK, 1)
-        copy_bank(bank_job(("w", MK, 2, 0)), "s")
+        copy_bank(bank_job(("x", 0, 1)), "v")
+        table_v(MK, 0)
         quantize(("x", 0))
-        copy_bank(bank_job(("w", MK, 2, 1)), "v")
+        copy_bank(bank_job(("w", MK, 2, 0)), "s")
+        spread_bias(MV, 0)
+        copy_bank(bank_job(("w", MK, 2, 1)), "s")
+        table_v(MK, 1)
+        tangents()
         copy_bank(bank_job(("w", MK, 3, 0)), "s")
+        spread_bias(MV, 1)
         copy_bank(bank_job(("w", MK, 3, 1)), "s")
+        multiply(MK, 0, 0)
+        multiply(MK, 1, 0)
         quantize(("w", MK, 1, 0))
         quantize(("w", MK, 1, 1))
+        add_bias(MK, 0, 0)
+        add_bias(MK, 1, 0)
+        copy_bank(bank_job(("x", 1, 0)), "s")
+        copy_bank(bank_job(("x", 1, 1)), "s")
+        multiply(MK, 0, 1)
+        multiply(MK, 1, 1)
+        quantize(("x", 1))
+        add_bias(MK, 0, 1)
+        add_bias(MK, 1, 1)
+        scale_tan(MK, 0, False)
+        copy_bank(bank_job(("x", 2, 0)), "s")
+        copy_bank(bank_job(("x", 2, 1)), "s")
+        scale_tan(MK, 1, False)
+        multiply(MK, 2, 0)
+        multiply(MK, 2, 1)
+        rotate_upper_v(MK, 0)
+        rotate_g(MK, 0, False)
 
-        units = [("x", 1), ("w", MQ, 0, 0), ("x", 2), ("w", MQ, 0, 1), ("x", 3), ("w", MQ, 1, 0), ("w", MQ, 1, 1)]
-        units += [("w", MV, h, g) for h in range(2) for g in range(2)]
-        slots = [(MK, n) for n in range(8)] + [(MQ, n) for n in range(4)]
-        for n in range(4):
-            slots += [(MQ, 4 + n), (MV, n)]
-        slots += [(MV, n) for n in range(4, 8)]
+        wq = [("w", MQ, h, g) for h in range(2) for g in range(2)]
+        wv = [("w", MV, h, g) for h in range(2) for g in range(2)]
         table_halves = [(m, a, j) for m, a in ((MK, 2), (MK, 3), (MQ, 0), (MQ, 1), (MQ, 2), (MQ, 3)) for j in range(2)]
-        ALL_G_FROM = 12
+        steps = PLAN(wq, wv)
 
-        def at(seq, i):
-            return seq[i] if 0 <= i < len(seq) else None
+        def units_at(s):
+            return steps[s][0] if 0 <= s < len(steps) else []
 
-        def store_delay(s):
-            if slots[s][0] == MV:
-                return 2
-            return 5 if s >= ALL_G_FROM else 3
+        def tile_at(s):
+            return steps[s][1] if 0 <= s < len(steps) else None
 
-        for s in range(len(slots) + 5):
-            unit = at(units, s)
-            if at(table_halves, s):
-                table_s(*table_halves[s])
-            if unit:
-                for job in unit_jobs(unit):
-                    copy_bank(bank_job(job), "s")
-            if at(slots, s):
-                multiply(*slots[s])
-            prev = at(slots, s - 1)
+        for s in range(3, len(steps) + 6):
+            jobs = [job for unit in units_at(s) for job in unit_jobs(unit)]
+            prev = tile_at(s - 1)
+            prev2 = tile_at(s - 2)
+            cur = tile_at(s)
+            first = [bank_job(job) for job in jobs[:2]]
+            heavy = len(jobs) > 2
+            for bank in first[:1 if heavy and VCOPY == 1 else 2]:
+                copy_bank(bank, "s")
             if prev:
-                add_bias(*prev)
-                if prev[0] != MV:
-                    scale_tan(*prev, s - 1 >= ALL_G_FROM)
-            if at(units, s - 1):
-                quantize(units[s - 1])
-            prev2 = at(slots, s - 2)
-            if prev2 and prev2[0] != MV and s - 2 < ALL_G_FROM:
+                add_bias(*prev, 0)
+                add_bias(*prev, 1)
+            if heavy and VCOPY == 1:
+                copy_bank(first[1], "v")
+            if SPLIT and len(jobs) > 2:
+                multiply(*cur, 0)
+            second = [bank_job(job) for job in jobs[2:]]
+            if second and VCOPY == 2:
+                copy_bank(second[0], "v")
+                second = second[1:]
+            if prev and prev[0] != MV:
+                scale_tan(*prev, ONG(*prev))
+            for bank in second:
+                copy_bank(bank, "s")
+            for unit in units_at(s - 1)[:-1 if OQ else None]:
+                quantize(unit)
+            if prev2 and prev2[0] != MV and not ONG(*prev2):
                 rotate_upper_v(*prev2)
                 rotate_g(*prev2, False)
-            if prev and prev[0] != MV and s - 1 >= ALL_G_FROM:
+            for unit in units_at(s - 1)[-1:] if OQ else []:
+                quantize(unit)
+            for t in table_halves[TAB(s):TAB(s + 1)]:
+                table_s(*t)
+            if cur:
+                if not (SPLIT and len(jobs) > 2):
+                    multiply(*cur, 0)
+                multiply(*cur, 1)
+            if prev and prev[0] != MV and ONG(*prev):
                 rotate_g(*prev, True)
-            for r in range(len(slots)):
-                if r + store_delay(r) == s:
-                    store(*slots[r])
+            for r in range(len(steps)):
+                if max(3, r + DELAY(*tile_at(r))) == s:
+                    store(*tile_at(r), 2 if r == len(steps) - 1 else 1)

@@ -12,220 +12,199 @@ BF16 = mybir.dt.bfloat16
 I32 = mybir.dt.int32
 U32 = mybir.dt.uint32
 U8 = mybir.dt.uint8
-MX = mybir.dt.float8_e5m2_x4
+E5M2X4 = mybir.dt.float8_e5m2_x4
 ALU = mybir.AluOpType
 ACT = mybir.ActivationFunctionType
 
 P = 128
-HALF = 512
+CHUNK = 2 * P
+HALF = E // 2
+PASS_WORDS = 256
+ROPE_BASE = 10000.0
 MK, MQ, MV = 0, 1, 2
-X_CHUNKS = [(0, 0), (1, 0), (0, 1), (1, 1)]
+N_TILES = B * S // P
+N_ANGLES = S // P
+X_CHUNKS = [(b, c) for c in range(S // CHUNK) for b in range(B)]
 
-
-def LOADS(load_w, load_x):
-    for c in "x2 q0 q1 x3 q2 q3 v0 v1 v2 v3".split():
-        if c[0] == "x":
-            load_x(int(c[1]))
-        else:
-            load_w(MQ if c[0] == "q" else MV, int(c[1]))
-
-
-def PLAN(wq, wv):
-    tiles = [({"k": MK, "q": MQ, "v": MV}[c[0]], int(c[1])) for c in "k0 k1 k2 k3 k4 k5 k6 k7 q0 q1 q2 v0 q3 v1 q4 v2 q5 v3 q6 v4 q7 v5 v6 v7".split()]
-    units = [[("x", int(u[1])) if u[0] == "x" else (wq if u[0] == "q" else wv)[int(u[1])] for u in c.split(",") if u != "-"] for c in "- - x2 q0 x3,q1 q2 q3 v0 v1 v2 v3".split()]
-    return [(units[i] if i < len(units) else [], t) for i, t in enumerate(tiles)]
-
-
-def ONG(m, n):
-    return (m, n) in [(MQ, 2), (MQ, 3), (MQ, 4), (MQ, 5), (MQ, 6), (MQ, 7)]
-
-
-def TAB(s):
-    return min(12, 2 * (s - 3) if s < 7 else s + 1)
-
-
-def DELAY(m, n):
-    return 1 if m == MV else (5 if ONG(m, n) else 3)
-
-
-SPLIT = False
-VCOPY = 0
-OQ = 1
+STAGE_BUFS = 4
+OUT_BUFS = 11
+TAN_BUFS = 4
+PSUM_BUFS = 4
+Q_ALL_ON_GPSIMD = 2
+STORE_LAG_V, STORE_LAG_SHARED, STORE_LAG_GPSIMD = 1, 3, 5
+FIRST_STEP = 3
+LAST_DOUBLE_TABLE_STEP = 6
 
 
 def tile_attention_kernel(tc, x, Wk, bk, Wq, bq, Wv, bv, out_0, out_1, out_2):
     nc = tc.nc
-    weights = [Wk, Wq, Wv]
     biases = [bk, bq, bv]
     outs = [o.rearrange("b (c p j) e -> b c j p e", p=P, j=2) for o in (out_0, out_1, out_2)]
     x_rows = x.rearrange("b (c p j) d -> b c p j d", p=P, j=2)
-    w_rows = [w.rearrange("(c p j) d -> c p j d", p=P, j=2) for w in weights]
+    w_rows = [w.rearrange("(c p j) d -> c p j d", p=P, j=2) for w in (Wk, Wq, Wv)]
 
     with ExitStack() as ctx:
         keep = ctx.enter_context(tc.tile_pool(name="keep", bufs=1))
-        stage = ctx.enter_context(tc.tile_pool(name="stage", bufs=4))
-        ypool = ctx.enter_context(tc.tile_pool(name="ypool", bufs=8))
-        apool = ctx.enter_context(tc.tile_pool(name="apool", bufs=4))
-        tpsum = ctx.enter_context(tc.psum_pool(name="tpsum", bufs=4))
-        mpsum = ctx.enter_context(tc.psum_pool(name="mpsum", bufs=4))
+        stage = ctx.enter_context(tc.tile_pool(name="stage", bufs=STAGE_BUFS))
+        ypool = ctx.enter_context(tc.tile_pool(name="ypool", bufs=OUT_BUFS))
+        tanpool = ctx.enter_context(tc.tile_pool(name="tanpool", bufs=TAN_BUFS))
+        tpsum = ctx.enter_context(tc.psum_pool(name="tpsum", bufs=PSUM_BUFS))
+        mpsum = ctx.enter_context(tc.psum_pool(name="mpsum", bufs=PSUM_BUFS))
         ctx.enter_context(tc.manual_schedule())
 
-        brows = keep.tile([P, E], BF16, name="brows")
-        nc.vector.memset(brows[:].bitcast(I32), 0)
-        for m in range(3):
-            nc.scalar.dma_start(out=brows[m:m + 1, :], in_=biases[m].rearrange("(o e) -> o e", o=1))
+        bias_rows = keep.tile([P, E], BF16, name="bias_rows")
+        nc.vector.memset(bias_rows[:].bitcast(I32), 0)
 
         raw = {}
 
-        def load(key, src, pieces=1):
-            t = keep.tile([P, 2, D], BF16, name="raw_%s_%d" % key)
-            raw[key] = t
-            w = D // pieces
+        def load(key, src, pieces):
+            raw[key] = keep.tile([P, 2, D], BF16, name="raw_%s_%d" % key)
+            width = D // pieces
             for i in range(pieces):
-                nc.sync.dma_start(out=t[:, :, i * w:(i + 1) * w], in_=src[:, :, i * w:(i + 1) * w])
+                cols = slice(i * width, (i + 1) * width)
+                nc.sync.dma_start(out=raw[key][:, :, cols], in_=src[:, :, cols])
 
         def load_w(m, c, pieces=1):
             load(("w%d" % m, c), w_rows[m][c], pieces)
 
-        def load_x(n):
-            load(("x", n), x_rows[X_CHUNKS[n][0], X_CHUNKS[n][1]])
+        def load_x(q):
+            load(("x", q), x_rows[X_CHUNKS[q][0], X_CHUNKS[q][1]], 1)
 
-        load_w(MK, 0, 2)
+        load_w(MK, 0, pieces=2)
+        for m in range(3):
+            nc.sync.dma_start(out=bias_rows[m:m + 1, :], in_=biases[m].rearrange("(o e) -> o e", o=1))
         load_w(MK, 1)
         load_x(0)
         load_w(MK, 2)
         load_w(MK, 3)
         load_x(1)
-        LOADS(load_w, load_x)
-
+        load_x(2)
+        load_w(MQ, 0)
+        load_w(MQ, 1)
+        load_x(3)
+        load_w(MQ, 2)
+        load_w(MQ, 3)
+        for c in range(E // CHUNK):
+            load_w(MV, c)
 
         ident = keep.tile([P, P], F32, name="ident")
-        sel = keep.tile([P, 4], BF16, name="sel")
-        pos = keep.tile([P, 4], F32, name="pos")
-        base = keep.tile([P, 4], F32, name="base")
-        expo = keep.tile([P, 4], F32, name="expo")
-        invf = keep.tile([P, 4], F32, name="invf")
-        nc.vector.memset(base[:], 10000.0)
+        selector = keep.tile([P, len(biases)], BF16, name="selector")
+        pos = keep.tile([P, N_ANGLES], F32, name="pos")
+        base = keep.tile([P, N_ANGLES], F32, name="base")
+        expo = keep.tile([P, N_ANGLES], F32, name="expo")
+        inv_freq = keep.tile([P, N_ANGLES], F32, name="inv_freq")
+        nc.vector.memset(base[:], ROPE_BASE)
         nc.vector.memset(ident[:], 0.0)
-        nc.gpsimd.iota(pos[:], pattern=[[256, 2], [1, 2]], base=0, channel_multiplier=2,
+        nc.gpsimd.iota(pos[:], pattern=[[CHUNK, S // CHUNK], [1, 2]], base=0, channel_multiplier=2,
                        allow_small_or_imprecise_dtypes=True)
         nc.gpsimd.tensor_scalar(expo[:], pos[:], -2.0 / E, 0.0, op0=ALU.mult, op1=ALU.add)
-        nc.gpsimd.tensor_tensor(invf[:], base[:], expo[:], op=ALU.pow)
+        nc.gpsimd.tensor_tensor(inv_freq[:], base[:], expo[:], op=ALU.pow)
         make_identity(nc, ident[:], nomemset=True)
 
-        turns = keep.tile([P, 8], F32, name="turns")
-        whole = keep.tile([P, 8], I32, name="whole")
-        frac = keep.tile([P, 8], F32, name="frac")
-        sincos = keep.tile([P, 8], F32, name="sincos")
-        rcos = keep.tile([P, 4], F32, name="rcos")
-        tan = keep.tile([P, 4], F32, name="tan")
-        ntan = keep.tile([P, 4], F32, name="ntan")
-        nc.vector.scalar_tensor_tensor(turns[:, 0:4], invf[:], 1.0 / (2.0 * math.pi), pos[:], op0=ALU.mult, op1=ALU.mult)
-        nc.vector.tensor_scalar(turns[:, 4:8], turns[:, 0:4], 0.25, None, op0=ALU.add)
+        sin_cols, cos_cols = slice(0, N_ANGLES), slice(N_ANGLES, 2 * N_ANGLES)
+        turns = keep.tile([P, 2 * N_ANGLES], F32, name="turns")
+        whole = keep.tile([P, 2 * N_ANGLES], I32, name="whole")
+        frac = keep.tile([P, 2 * N_ANGLES], F32, name="frac")
+        sincos = keep.tile([P, 2 * N_ANGLES], F32, name="sincos")
+        rcos = keep.tile([P, N_ANGLES], F32, name="rcos")
+        tan = keep.tile([P, N_ANGLES], F32, name="tan")
+        ntan = keep.tile([P, N_ANGLES], F32, name="ntan")
+        nc.vector.scalar_tensor_tensor(turns[:, sin_cols], inv_freq[:], 1.0 / (2.0 * math.pi), pos[:],
+                                       op0=ALU.mult, op1=ALU.mult)
+        nc.vector.tensor_scalar(turns[:, cos_cols], turns[:, sin_cols], 0.25, None, op0=ALU.add)
         nc.vector.tensor_copy(whole[:], turns[:])
-        nc.vector.tensor_copy(sel[:], ident[:, 0:4])
+        nc.vector.tensor_copy(selector[:], ident[:, 0:len(biases)])
         nc.vector.tensor_tensor(frac[:], turns[:], whole[:], op=ALU.subtract)
         nc.scalar.activation(sincos[:], frac[:], ACT.Sin, scale=2.0 * math.pi)
 
+        def cos_of(a):
+            return sincos[:, N_ANGLES + a:N_ANGLES + a + 1]
+
         def tangents():
-            nc.vector.reciprocal(rcos[:], sincos[:, 4:8])
-            nc.vector.tensor_tensor(tan[:], sincos[:, 0:4], rcos[:], op=ALU.mult)
-            nc.vector.scalar_tensor_tensor(ntan[:], sincos[:, 0:4], -1.0, rcos[:], op0=ALU.mult, op1=ALU.mult)
+            nc.vector.reciprocal(rcos[:], sincos[:, cos_cols])
+            nc.vector.tensor_tensor(tan[:], sincos[:, sin_cols], rcos[:], op=ALU.mult)
+            nc.vector.scalar_tensor_tensor(ntan[:], sincos[:, sin_cols], -1.0, rcos[:], op0=ALU.mult, op1=ALU.mult)
 
-        bias_sb = {}
-
-        bias_ps = {}
+        bias_banks = {}
+        bias_tiles = {}
+        tables = {}
 
         def spread_bias(m, j):
             if j == 0:
-                bias_ps[m] = mpsum.tile([P, E], BF16, name="mb", tag="mb")
-            pb = bias_ps[m]
-            cols = brows[:, j * HALF:(j + 1) * HALF] if m == MV else brows[:, j:E:2]
-            nc.tensor.matmul(pb[:, j * HALF:(j + 1) * HALF], lhsT=sel[:, m:m + 1].to_broadcast([P, P]),
-                             rhs=cols, start=True, stop=True)
+                bias_banks[m] = mpsum.tile([P, E], BF16, name="product", tag="product")
+            src = bias_rows[:, j * HALF:(j + 1) * HALF] if m == MV else bias_rows[:, j:E:2]
+            nc.tensor.matmul(bias_banks[m][:, j * HALF:(j + 1) * HALF], lhsT=selector[:, m:m + 1].to_broadcast([P, P]),
+                             rhs=src, start=True, stop=True)
             if j == 1:
-                bias_sb[m] = keep.tile([P, E], BF16, name="bias%d" % m)
-                nc.scalar.copy(bias_sb[m][:], pb[:])
+                bias_tiles[m] = keep.tile([P, E], BF16, name="bias%d" % m)
+                nc.scalar.copy(bias_tiles[m][:], bias_banks[m][:])
 
-        def copy_on(eng, out, in_):
-            if eng == "v":
-                nc.vector.tensor_copy(out, in_)
-            else:
-                nc.scalar.copy(out, in_)
-
-        tables = {}
-
-        def table_tile(m, a):
+        def table(m, a):
             if (m, a) not in tables:
-                tables[(m, a)] = keep.tile([P, E], F32, name="cb%d_%d" % (m, a))
+                tables[(m, a)] = keep.tile([P, E], F32, name="table%d_%d" % (m, a))
             return tables[(m, a)]
 
-        def table_v(m, a):
-            nc.vector.tensor_scalar(table_tile(m, a)[:], bias_sb[m][:], sincos[:, 4 + a:5 + a], None, op0=ALU.mult)
+        def table_on_vector(m, a):
+            nc.vector.tensor_scalar(table(m, a)[:], bias_tiles[m][:], cos_of(a), None, op0=ALU.mult)
 
-        def table_g(m, a):
-            nc.gpsimd.tensor_scalar(table_tile(m, a)[:], bias_sb[m][:], sincos[:, 4 + a:5 + a], 0.0, op0=ALU.mult, op1=ALU.add)
-
-        def table_s(m, a, j):
+        def half_table_on_scalar(m, a, j):
             cols = slice(j * HALF, (j + 1) * HALF)
-            nc.scalar.activation(table_tile(m, a)[:, cols], bias_sb[m][:, cols], ACT.Copy, scale=sincos[:, 4 + a:5 + a])
+            nc.scalar.activation(table(m, a)[:, cols], bias_tiles[m][:, cols], ACT.Copy, scale=cos_of(a))
 
         staged = {}
         codes = {}
         scales = {}
 
-        def transpose_bank(key, g):
-            bank = tpsum.tile([P, 2, 2, P], F32, name="tb", tag="tb")
-            for j in range(2):
-                words = raw[key][:, j, :].bitcast(F32)
-                for u in range(2):
-                    nc.tensor.transpose(bank[:, j, u, :], words[:, 256 * g + u:256 * (g + 1):2], ident[:])
-            return bank
-
-        def stage_tile(unit):
+        def staged_words(unit):
             if unit not in staged:
                 staged[unit] = stage.tile([P, 4 * HALF], BF16, name="staged", tag="staged", align_bytes=64)
             return staged[unit][:].bitcast(F32)
 
-        def bank_job(job):
-            if job[0] == "w":
-                m, c, g = job[1:]
-                bank = transpose_bank(("w%d" % m, c), g)
-                dst = stage_tile(("w", m, c // 2, g)).rearrange("p (j c r u) -> p j c r u", j=2, c=2, u=2)[:, :, c % 2, :, :]
-            else:
-                n, g = job[1:]
-                bank = transpose_bank(("x", n), g)
-                dst = stage_tile(("x", n)).rearrange("p (g j r u) -> p g j r u", g=2, j=2, u=2)[:, g, :, :, :]
-            return bank, dst
+        def transpose_pass(key, g):
+            bank = tpsum.tile([P, 2, 2, P], F32, name="turned", tag="turned")
+            for j in range(2):
+                words = raw[key][:, j, :].bitcast(F32)
+                for u in range(2):
+                    nc.tensor.transpose(bank[:, j, u, :], words[:, PASS_WORDS * g + u:PASS_WORDS * (g + 1):2], ident[:])
+            return bank[:].rearrange("p j u r -> p j r u")
 
-        def copy_bank(bank_dst, eng):
-            bank, dst = bank_dst
-            copy_on(eng, dst, bank[:].rearrange("p j u r -> p j r u"))
+        def turn_w(m, c, g):
+            bank = transpose_pass(("w%d" % m, c), g)
+            dst = staged_words(("w", m, c // 2, g)).rearrange("p (j c r u) -> p j c r u", j=2, c=2, u=2)
+            return dst[:, :, c % 2, :, :], bank
+
+        def turn_x(q, g):
+            bank = transpose_pass(("x", q), g)
+            dst = staged_words(("x", q)).rearrange("p (g j r u) -> p g j r u", g=2, j=2, u=2)
+            return dst[:, g, :, :, :], bank
+
+        def turn_unit(unit):
+            if unit[0] == "w":
+                m, h, g = unit[1:]
+                return [turn_w(m, 2 * h + c, g) for c in range(2)]
+            return [turn_x(unit[1], g) for g in range(2)]
 
         def quantize(unit):
             name = "_".join(str(v) for v in unit)
             codes[unit] = keep.tile([P, HALF], U32, name="codes_" + name, align_bytes=64)
             scales[unit] = keep.tile([P, HALF], U8, name="scales_" + name, align_bytes=64)
-            nc.vector.quantize_mx(out=codes[unit][:].bitcast(MX), scales=scales[unit][:], in_=staged[unit][:])
-
-        def unit_jobs(unit):
-            if unit[0] == "w":
-                return [("w", unit[1], 2 * unit[2] + c, unit[3]) for c in range(2)]
-            return [("x", unit[1], g) for g in range(2)]
+            nc.vector.quantize_mx(out=codes[unit][:].bitcast(E5M2X4), scales=scales[unit][:], in_=staged[unit][:])
 
         banks = {}
         ys = {}
-        scaled = {}
+        tan_ys = {}
 
         def multiply(m, n, h):
-            xu = ("x", n // 2)
-            bank = mpsum.tile([P, HALF], F32, name="mb", tag="mb")
+            x_unit = ("x", n // 2)
+            bank = mpsum.tile([P, HALF], F32, name="product", tag="product")
             banks[(m, n, h)] = bank
             for g in range(2):
-                cols = slice(256 * g + P * (n % 2), 256 * g + P * (n % 2) + P)
-                wu = ("w", m, h, g)
-                nc.tensor.matmul_mx(out=bank[:], lhsT=codes[xu][:, cols].bitcast(MX), lhsT_scale=scales[xu][:, cols],
-                                    rhs=codes[wu][:].bitcast(MX), rhs_scale=scales[wu][:],
+                first = CHUNK * g + P * (n % 2)
+                tokens = slice(first, first + P)
+                w_unit = ("w", m, h, g)
+                nc.tensor.matmul_mx(out=bank[:], lhsT=codes[x_unit][:, tokens].bitcast(E5M2X4),
+                                    lhsT_scale=scales[x_unit][:, tokens],
+                                    rhs=codes[w_unit][:].bitcast(E5M2X4), rhs_scale=scales[w_unit][:],
                                     start=(g == 0), stop=(g == 1))
 
         def angle_col(n):
@@ -240,135 +219,138 @@ def tile_attention_kernel(tc, x, Wk, bk, Wq, bq, Wv, bv, out_0, out_1, out_2):
                 cols = slice(h * HALF, (h + 1) * HALF)
                 nc.vector.tensor_tensor(y[:, cols].rearrange("p (r j) -> p r j", j=2),
                                         bank[:].rearrange("p (j r) -> p r j", j=2),
-                                        bias_sb[m][:, cols].rearrange("p (r j) -> p r j", j=2), op=ALU.add)
+                                        bias_tiles[m][:, cols].rearrange("p (r j) -> p r j", j=2), op=ALU.add)
             else:
                 a = angle_col(n)
                 nc.vector.scalar_tensor_tensor(
                     y[:].rearrange("p (j h r) -> p j h r", j=2, h=2)[:, :, h, :],
                     bank[:].rearrange("p (j r) -> p j r", j=2),
-                    sincos[:, 4 + a:5 + a],
+                    cos_of(a),
                     tables[(m, a)][:].rearrange("p (j h r) -> p j h r", j=2, h=2)[:, :, h, :],
                     op0=ALU.mult, op1=ALU.add)
 
-        def scale_tan(m, n, both):
-            t = apool.tile([P, E], F32, name="ty", tag="ty")
-            scaled[(m, n)] = t
+        def all_on_gpsimd(m, n):
+            return m == MQ and n >= Q_ALL_ON_GPSIMD
+
+        def scale_by_tan(m, n):
+            tan_y = tanpool.tile([P, E], F32, name="tan_y", tag="tan_y")
+            tan_ys[(m, n)] = tan_y
             a = angle_col(n)
             y = ys[(m, n)]
-            nc.scalar.activation(t[:, 0:HALF], y[:, HALF:E], ACT.Copy, scale=ntan[:, a:a + 1])
-            if both:
-                nc.scalar.activation(t[:, HALF:E], y[:, 0:HALF], ACT.Copy, scale=tan[:, a:a + 1])
+            nc.scalar.activation(tan_y[:, 0:HALF], y[:, HALF:E], ACT.Copy, scale=ntan[:, a:a + 1])
+            if all_on_gpsimd(m, n):
+                nc.scalar.activation(tan_y[:, HALF:E], y[:, 0:HALF], ACT.Copy, scale=tan[:, a:a + 1])
 
-        def rotate_upper_v(m, n):
+        def rotate_shared(m, n):
             y = ys[(m, n)]
             a = angle_col(n)
-            nc.vector.scalar_tensor_tensor(y[:, HALF:E], y[:, 0:HALF], tan[:, a:a + 1], y[:, HALF:E], op0=ALU.mult, op1=ALU.add)
+            nc.vector.scalar_tensor_tensor(y[:, HALF:E], y[:, 0:HALF], tan[:, a:a + 1], y[:, HALF:E],
+                                           op0=ALU.mult, op1=ALU.add)
+            nc.gpsimd.tensor_tensor(y[:, 0:HALF], y[:, 0:HALF], tan_ys[(m, n)][:, 0:HALF], op=ALU.add)
 
-        def rotate_g(m, n, both):
+        def rotate_on_gpsimd(m, n):
             y = ys[(m, n)]
-            cols = slice(0, E if both else HALF)
-            nc.gpsimd.tensor_tensor(y[:, cols], y[:, cols], scaled[(m, n)][:, cols], op=ALU.add)
+            nc.gpsimd.tensor_tensor(y[:], y[:], tan_ys[(m, n)][:], op=ALU.add)
 
-        def store(m, n, pieces=1):
+        def store(m, n, pieces):
             b, c = X_CHUNKS[n // 2]
-            w = E // pieces
+            width = E // pieces
             for i in range(pieces):
-                nc.sync.dma_start(out=outs[m][b, c, n % 2][:, i * w:(i + 1) * w], in_=ys[(m, n)][:, i * w:(i + 1) * w])
+                cols = slice(i * width, (i + 1) * width)
+                nc.sync.dma_start(out=outs[m][b, c, n % 2][:, cols], in_=ys[(m, n)][:, cols])
 
-        copy_bank(bank_job(("w", MK, 0, 0)), "s")
+        nc.scalar.copy(*turn_w(MK, 0, 0))
         spread_bias(MK, 0)
         spread_bias(MK, 1)
-        copy_bank(bank_job(("w", MK, 0, 1)), "v")
-        copy_bank(bank_job(("w", MK, 1, 0)), "s")
+        nc.vector.tensor_copy(*turn_w(MK, 0, 1))
+        nc.scalar.copy(*turn_w(MK, 1, 0))
         spread_bias(MQ, 0)
-        copy_bank(bank_job(("w", MK, 1, 1)), "v")
+        nc.vector.tensor_copy(*turn_w(MK, 1, 1))
         quantize(("w", MK, 0, 0))
-        copy_bank(bank_job(("x", 0, 0)), "s")
+        nc.scalar.copy(*turn_x(0, 0))
         spread_bias(MQ, 1)
         quantize(("w", MK, 0, 1))
-        copy_bank(bank_job(("x", 0, 1)), "v")
-        table_v(MK, 0)
+        nc.vector.tensor_copy(*turn_x(0, 1))
+        table_on_vector(MK, 0)
         quantize(("x", 0))
-        copy_bank(bank_job(("w", MK, 2, 0)), "s")
+        nc.scalar.copy(*turn_w(MK, 2, 0))
         spread_bias(MV, 0)
-        copy_bank(bank_job(("w", MK, 2, 1)), "s")
-        table_v(MK, 1)
+        nc.scalar.copy(*turn_w(MK, 2, 1))
+        table_on_vector(MK, 1)
         tangents()
-        copy_bank(bank_job(("w", MK, 3, 0)), "s")
+        nc.scalar.copy(*turn_w(MK, 3, 0))
         spread_bias(MV, 1)
-        copy_bank(bank_job(("w", MK, 3, 1)), "s")
+        nc.scalar.copy(*turn_w(MK, 3, 1))
         multiply(MK, 0, 0)
         multiply(MK, 1, 0)
         quantize(("w", MK, 1, 0))
         quantize(("w", MK, 1, 1))
         add_bias(MK, 0, 0)
         add_bias(MK, 1, 0)
-        copy_bank(bank_job(("x", 1, 0)), "s")
-        copy_bank(bank_job(("x", 1, 1)), "s")
+        nc.scalar.copy(*turn_x(1, 0))
+        nc.scalar.copy(*turn_x(1, 1))
         multiply(MK, 0, 1)
         multiply(MK, 1, 1)
         quantize(("x", 1))
         add_bias(MK, 0, 1)
         add_bias(MK, 1, 1)
-        scale_tan(MK, 0, False)
-        copy_bank(bank_job(("x", 2, 0)), "s")
-        copy_bank(bank_job(("x", 2, 1)), "s")
-        scale_tan(MK, 1, False)
+        scale_by_tan(MK, 0)
+        nc.scalar.copy(*turn_x(2, 0))
+        nc.scalar.copy(*turn_x(2, 1))
+        scale_by_tan(MK, 1)
         multiply(MK, 2, 0)
         multiply(MK, 2, 1)
-        rotate_upper_v(MK, 0)
-        rotate_g(MK, 0, False)
+        rotate_shared(MK, 0)
 
         wq = [("w", MQ, h, g) for h in range(2) for g in range(2)]
         wv = [("w", MV, h, g) for h in range(2) for g in range(2)]
-        table_halves = [(m, a, j) for m, a in ((MK, 2), (MK, 3), (MQ, 0), (MQ, 1), (MQ, 2), (MQ, 3)) for j in range(2)]
-        steps = PLAN(wq, wv)
+        units = [[], [], [("x", 2)], [wq[0]], [("x", 3), wq[1]]] + [[unit] for unit in wq[2:] + wv]
+        q_before_v = len(units) - N_TILES
+        tiles = [(MK, n) for n in range(N_TILES)] + [(MQ, n) for n in range(q_before_v)]
+        for n in range(N_TILES):
+            tiles += [(MV, n)] + ([(MQ, q_before_v + n)] if q_before_v + n < N_TILES else [])
+        half_tables = [(m, a, j) for m in (MK, MQ) for a in range(N_ANGLES) for j in range(2) if (m, a) not in tables]
 
         def units_at(s):
-            return steps[s][0] if 0 <= s < len(steps) else []
+            return units[s] if s < len(units) else []
 
         def tile_at(s):
-            return steps[s][1] if 0 <= s < len(steps) else None
+            return tiles[s] if s < len(tiles) else None
 
-        for s in range(3, len(steps) + 6):
-            jobs = [job for unit in units_at(s) for job in unit_jobs(unit)]
-            prev = tile_at(s - 1)
-            prev2 = tile_at(s - 2)
-            cur = tile_at(s)
-            first = [bank_job(job) for job in jobs[:2]]
-            heavy = len(jobs) > 2
-            for bank in first[:1 if heavy and VCOPY == 1 else 2]:
-                copy_bank(bank, "s")
-            if prev:
-                add_bias(*prev, 0)
-                add_bias(*prev, 1)
-            if heavy and VCOPY == 1:
-                copy_bank(first[1], "v")
-            if SPLIT and len(jobs) > 2:
-                multiply(*cur, 0)
-            second = [bank_job(job) for job in jobs[2:]]
-            if second and VCOPY == 2:
-                copy_bank(second[0], "v")
-                second = second[1:]
-            if prev and prev[0] != MV:
-                scale_tan(*prev, ONG(*prev))
-            for bank in second:
-                copy_bank(bank, "s")
-            for unit in units_at(s - 1)[:-1 if OQ else None]:
+        def rotated(tile):
+            return tile is not None and tile[0] != MV
+
+        def store_step(s):
+            if tiles[s][0] == MV:
+                return s + STORE_LAG_V
+            return s + (STORE_LAG_GPSIMD if all_on_gpsimd(*tiles[s]) else STORE_LAG_SHARED)
+
+        for s in range(FIRST_STEP, max(store_step(r) for r in range(len(tiles))) + 1):
+            now, last, before_last = tile_at(s), tile_at(s - 1), tile_at(s - 2)
+            for dst, bank in [job for unit in units_at(s)[:1] for job in turn_unit(unit)]:
+                nc.scalar.copy(dst, bank)
+            if last:
+                add_bias(*last, 0)
+                add_bias(*last, 1)
+            second_unit = [job for unit in units_at(s)[1:] for job in turn_unit(unit)]
+            if rotated(last):
+                scale_by_tan(*last)
+            for dst, bank in second_unit:
+                nc.scalar.copy(dst, bank)
+            for unit in units_at(s - 1)[:-1]:
                 quantize(unit)
-            if prev2 and prev2[0] != MV and not ONG(*prev2):
-                rotate_upper_v(*prev2)
-                rotate_g(*prev2, False)
-            for unit in units_at(s - 1)[-1:] if OQ else []:
+            if rotated(before_last) and not all_on_gpsimd(*before_last):
+                rotate_shared(*before_last)
+            for unit in units_at(s - 1)[-1:]:
                 quantize(unit)
-            for t in table_halves[TAB(s):TAB(s + 1)]:
-                table_s(*t)
-            if cur:
-                if not (SPLIT and len(jobs) > 2):
-                    multiply(*cur, 0)
-                multiply(*cur, 1)
-            if prev and prev[0] != MV and ONG(*prev):
-                rotate_g(*prev, True)
-            for r in range(len(steps)):
-                if max(3, r + DELAY(*tile_at(r))) == s:
-                    store(*tile_at(r), 2 if r == len(steps) - 1 else 1)
+            for job in half_tables[:2 if s <= LAST_DOUBLE_TABLE_STEP else 1]:
+                half_table_on_scalar(*job)
+                half_tables.remove(job)
+            if now:
+                multiply(*now, 0)
+                multiply(*now, 1)
+            if rotated(last) and all_on_gpsimd(*last):
+                rotate_on_gpsimd(*last)
+            for r in range(len(tiles)):
+                if store_step(r) == s:
+                    store(*tiles[r], 2 if r == len(tiles) - 1 else 1)

@@ -30,10 +30,9 @@ STAGE_BUFS = 4
 OUT_BUFS = 11
 TAN_BUFS = 4
 PSUM_BUFS = 4
-Q_ALL_ON_GPSIMD = 2
-STORE_LAG_V, STORE_LAG_SHARED, STORE_LAG_GPSIMD = 1, 3, 5
+STORE_LAG_V, STORE_LAG_K, STORE_LAG_Q = 1, 3, 5
 FIRST_STEP = 3
-LAST_DOUBLE_TABLE_STEP = 6
+SINGLE_TABLE_STEPS = (5, 6)
 
 
 def tile_attention_kernel(tc, x, Wk, bk, Wq, bq, Wv, bv, out_0, out_1, out_2):
@@ -229,16 +228,13 @@ def tile_attention_kernel(tc, x, Wk, bk, Wq, bq, Wv, bv, out_0, out_1, out_2):
                     tables[(m, a)][:].rearrange("p (j h r) -> p j h r", j=2, h=2)[:, :, h, :],
                     op0=ALU.mult, op1=ALU.add)
 
-        def all_on_gpsimd(m, n):
-            return m == MQ and n >= Q_ALL_ON_GPSIMD
-
         def scale_by_tan(m, n):
             tan_y = tanpool.tile([P, E], F32, name="tan_y", tag="tan_y")
             tan_ys[(m, n)] = tan_y
             a = angle_col(n)
             y = ys[(m, n)]
             nc.scalar.activation(tan_y[:, 0:HALF], y[:, HALF:E], ACT.Copy, scale=ntan[:, a:a + 1])
-            if all_on_gpsimd(m, n):
+            if m == MQ:
                 nc.scalar.activation(tan_y[:, HALF:E], y[:, 0:HALF], ACT.Copy, scale=tan[:, a:a + 1])
 
         def rotate_shared(m, n):
@@ -248,16 +244,13 @@ def tile_attention_kernel(tc, x, Wk, bk, Wq, bq, Wv, bv, out_0, out_1, out_2):
                                            op0=ALU.mult, op1=ALU.add)
             nc.gpsimd.tensor_tensor(y[:, 0:HALF], y[:, 0:HALF], tan_ys[(m, n)][:, 0:HALF], op=ALU.add)
 
-        def rotate_on_gpsimd(m, n):
+        def rotate_whole(engine, m, n):
             y = ys[(m, n)]
-            nc.gpsimd.tensor_tensor(y[:], y[:], tan_ys[(m, n)][:], op=ALU.add)
+            engine.tensor_tensor(y[:], y[:], tan_ys[(m, n)][:], op=ALU.add)
 
-        def store(m, n, pieces):
+        def store(m, n):
             b, c = X_CHUNKS[n // 2]
-            width = E // pieces
-            for i in range(pieces):
-                cols = slice(i * width, (i + 1) * width)
-                nc.sync.dma_start(out=outs[m][b, c, n % 2][:, cols], in_=ys[(m, n)][:, cols])
+            nc.sync.dma_start(out=outs[m][b, c, n % 2], in_=ys[(m, n)][:])
 
         nc.scalar.copy(*turn_w(MK, 0, 0))
         spread_bias(MK, 0)
@@ -291,8 +284,8 @@ def tile_attention_kernel(tc, x, Wk, bk, Wq, bq, Wv, bv, out_0, out_1, out_2):
         nc.scalar.copy(*turn_x(1, 1))
         multiply(MK, 0, 1)
         multiply(MK, 1, 1)
-        quantize(("x", 1))
         add_bias(MK, 0, 1)
+        quantize(("x", 1))
         add_bias(MK, 1, 1)
         scale_by_tan(MK, 0)
         nc.scalar.copy(*turn_x(2, 0))
@@ -304,11 +297,9 @@ def tile_attention_kernel(tc, x, Wk, bk, Wq, bq, Wv, bv, out_0, out_1, out_2):
 
         wq = [("w", MQ, h, g) for h in range(2) for g in range(2)]
         wv = [("w", MV, h, g) for h in range(2) for g in range(2)]
-        units = [[], [], [("x", 2)], [wq[0]], [("x", 3), wq[1]]] + [[unit] for unit in wq[2:] + wv]
-        q_before_v = len(units) - N_TILES
-        tiles = [(MK, n) for n in range(N_TILES)] + [(MQ, n) for n in range(q_before_v)]
-        for n in range(N_TILES):
-            tiles += [(MV, n)] + ([(MQ, q_before_v + n)] if q_before_v + n < N_TILES else [])
+        units = [[], [], [("x", 2)], wq[0:1], [("x", 3), wq[1]], wq[2:4], wv[0:1], wv[1:3], wv[3:4]]
+        tiles = [(MK, n) for n in range(N_TILES)] + [(m, n) for n in range(N_TILES) for m in (MQ, MV)]
+        last_q = (MQ, N_TILES - 1)
         half_tables = [(m, a, j) for m in (MK, MQ) for a in range(N_ANGLES) for j in range(2) if (m, a) not in tables]
 
         def units_at(s):
@@ -317,13 +308,10 @@ def tile_attention_kernel(tc, x, Wk, bk, Wq, bq, Wv, bv, out_0, out_1, out_2):
         def tile_at(s):
             return tiles[s] if s < len(tiles) else None
 
-        def rotated(tile):
-            return tile is not None and tile[0] != MV
-
         def store_step(s):
             if tiles[s][0] == MV:
                 return s + STORE_LAG_V
-            return s + (STORE_LAG_GPSIMD if all_on_gpsimd(*tiles[s]) else STORE_LAG_SHARED)
+            return s + (STORE_LAG_Q if tiles[s][0] == MQ else STORE_LAG_K)
 
         for s in range(FIRST_STEP, max(store_step(r) for r in range(len(tiles))) + 1):
             now, last, before_last = tile_at(s), tile_at(s - 1), tile_at(s - 2)
@@ -333,24 +321,26 @@ def tile_attention_kernel(tc, x, Wk, bk, Wq, bq, Wv, bv, out_0, out_1, out_2):
                 add_bias(*last, 0)
                 add_bias(*last, 1)
             second_unit = [job for unit in units_at(s)[1:] for job in turn_unit(unit)]
-            if rotated(last):
+            if last and last[0] != MV:
                 scale_by_tan(*last)
             for dst, bank in second_unit:
                 nc.scalar.copy(dst, bank)
             for unit in units_at(s - 1)[:-1]:
                 quantize(unit)
-            if rotated(before_last) and not all_on_gpsimd(*before_last):
+            if before_last and before_last[0] == MK:
                 rotate_shared(*before_last)
             for unit in units_at(s - 1)[-1:]:
                 quantize(unit)
-            for job in half_tables[:2 if s <= LAST_DOUBLE_TABLE_STEP else 1]:
+            for job in half_tables[:1 if s in SINGLE_TABLE_STEPS else 2]:
                 half_table_on_scalar(*job)
                 half_tables.remove(job)
             if now:
                 multiply(*now, 0)
                 multiply(*now, 1)
-            if rotated(last) and all_on_gpsimd(*last):
-                rotate_on_gpsimd(*last)
+            if last and last[0] == MQ and last != last_q:
+                rotate_whole(nc.gpsimd, *last)
+            if before_last == last_q:
+                rotate_whole(nc.vector, *last_q)
             for r in range(len(tiles)):
                 if store_step(r) == s:
-                    store(*tiles[r], 2 if r == len(tiles) - 1 else 1)
+                    store(*tiles[r])

import math
from contextlib import ExitStack

import concourse.mybir as mybir
from concourse.masks import make_identity

B, S, D, E = 2, 512, 1024, 1024
FLOPS = 2 * B * S * D * 3 * E

F32 = mybir.dt.float32
BF16 = mybir.dt.bfloat16
I32 = mybir.dt.int32
U32 = mybir.dt.uint32
U8 = mybir.dt.uint8
E5M2X4 = mybir.dt.float8_e5m2_x4
ALU = mybir.AluOpType
ACT = mybir.ActivationFunctionType

P = 128
CHUNK = 2 * P
HALF = E // 2
PASS_WORDS = 256
ROPE_BASE = 10000.0
MK, MQ, MV = 0, 1, 2
N_TILES = B * S // P
N_ANGLES = S // P
X_CHUNKS = [(b, c) for c in range(S // CHUNK) for b in range(B)]

STAGE_BUFS = 4
OUT_BUFS = 11
TAN_BUFS = 4
PSUM_BUFS = 4
STORE_LAG_V, STORE_LAG_K, STORE_LAG_Q = 1, 3, 5
FIRST_STEP = 3
SINGLE_TABLE_STEPS = (5, 6)


def tile_attention_kernel(tc, x, Wk, bk, Wq, bq, Wv, bv, out_0, out_1, out_2):
    nc = tc.nc
    biases = [bk, bq, bv]
    outs = [o.rearrange("b (c p j) e -> b c j p e", p=P, j=2) for o in (out_0, out_1, out_2)]
    x_rows = x.rearrange("b (c p j) d -> b c p j d", p=P, j=2)
    w_rows = [w.rearrange("(c p j) d -> c p j d", p=P, j=2) for w in (Wk, Wq, Wv)]

    with ExitStack() as ctx:
        keep = ctx.enter_context(tc.tile_pool(name="keep", bufs=1))
        stage = ctx.enter_context(tc.tile_pool(name="stage", bufs=STAGE_BUFS))
        ypool = ctx.enter_context(tc.tile_pool(name="ypool", bufs=OUT_BUFS))
        tanpool = ctx.enter_context(tc.tile_pool(name="tanpool", bufs=TAN_BUFS))
        tpsum = ctx.enter_context(tc.psum_pool(name="tpsum", bufs=PSUM_BUFS))
        mpsum = ctx.enter_context(tc.psum_pool(name="mpsum", bufs=PSUM_BUFS))
        ctx.enter_context(tc.manual_schedule())

        bias_rows = keep.tile([P, E], BF16, name="bias_rows")
        nc.vector.memset(bias_rows[:].bitcast(I32), 0)

        raw = {}

        def load(key, src, pieces):
            raw[key] = keep.tile([P, 2, D], BF16, name="raw_%s_%d" % key)
            width = D // pieces
            for i in range(pieces):
                cols = slice(i * width, (i + 1) * width)
                nc.sync.dma_start(out=raw[key][:, :, cols], in_=src[:, :, cols])

        def load_w(m, c, pieces=1):
            load(("w%d" % m, c), w_rows[m][c], pieces)

        def load_x(q):
            load(("x", q), x_rows[X_CHUNKS[q][0], X_CHUNKS[q][1]], 1)

        load_w(MK, 0, pieces=2)
        for m in range(3):
            nc.sync.dma_start(out=bias_rows[m:m + 1, :], in_=biases[m].rearrange("(o e) -> o e", o=1))
        load_w(MK, 1)
        load_x(0)
        load_w(MK, 2)
        load_w(MK, 3)
        load_x(1)
        load_x(2)
        load_w(MQ, 0)
        load_w(MQ, 1)
        load_x(3)
        load_w(MQ, 2)
        load_w(MQ, 3)
        for c in range(E // CHUNK):
            load_w(MV, c)

        ident = keep.tile([P, P], F32, name="ident")
        selector = keep.tile([P, len(biases)], BF16, name="selector")
        pos = keep.tile([P, N_ANGLES], F32, name="pos")
        base = keep.tile([P, N_ANGLES], F32, name="base")
        expo = keep.tile([P, N_ANGLES], F32, name="expo")
        inv_freq = keep.tile([P, N_ANGLES], F32, name="inv_freq")
        nc.vector.memset(base[:], ROPE_BASE)
        nc.vector.memset(ident[:], 0.0)
        nc.gpsimd.iota(pos[:], pattern=[[CHUNK, S // CHUNK], [1, 2]], base=0, channel_multiplier=2,
                       allow_small_or_imprecise_dtypes=True)
        nc.gpsimd.tensor_scalar(expo[:], pos[:], -2.0 / E, 0.0, op0=ALU.mult, op1=ALU.add)
        nc.gpsimd.tensor_tensor(inv_freq[:], base[:], expo[:], op=ALU.pow)
        make_identity(nc, ident[:], nomemset=True)

        sin_cols, cos_cols = slice(0, N_ANGLES), slice(N_ANGLES, 2 * N_ANGLES)
        turns = keep.tile([P, 2 * N_ANGLES], F32, name="turns")
        whole = keep.tile([P, 2 * N_ANGLES], I32, name="whole")
        frac = keep.tile([P, 2 * N_ANGLES], F32, name="frac")
        sincos = keep.tile([P, 2 * N_ANGLES], F32, name="sincos")
        rcos = keep.tile([P, N_ANGLES], F32, name="rcos")
        tan = keep.tile([P, N_ANGLES], F32, name="tan")
        ntan = keep.tile([P, N_ANGLES], F32, name="ntan")
        nc.vector.scalar_tensor_tensor(turns[:, sin_cols], inv_freq[:], 1.0 / (2.0 * math.pi), pos[:],
                                       op0=ALU.mult, op1=ALU.mult)
        nc.vector.tensor_scalar(turns[:, cos_cols], turns[:, sin_cols], 0.25, None, op0=ALU.add)
        nc.vector.tensor_copy(whole[:], turns[:])
        nc.vector.tensor_copy(selector[:], ident[:, 0:len(biases)])
        nc.vector.tensor_tensor(frac[:], turns[:], whole[:], op=ALU.subtract)
        nc.scalar.activation(sincos[:], frac[:], ACT.Sin, scale=2.0 * math.pi)

        def cos_of(a):
            return sincos[:, N_ANGLES + a:N_ANGLES + a + 1]

        def tangents():
            nc.vector.reciprocal(rcos[:], sincos[:, cos_cols])
            nc.vector.tensor_tensor(tan[:], sincos[:, sin_cols], rcos[:], op=ALU.mult)
            nc.vector.scalar_tensor_tensor(ntan[:], sincos[:, sin_cols], -1.0, rcos[:], op0=ALU.mult, op1=ALU.mult)

        bias_banks = {}
        bias_tiles = {}
        tables = {}

        def spread_bias(m, j):
            if j == 0:
                bias_banks[m] = mpsum.tile([P, E], BF16, name="product", tag="product")
            src = bias_rows[:, j * HALF:(j + 1) * HALF] if m == MV else bias_rows[:, j:E:2]
            nc.tensor.matmul(bias_banks[m][:, j * HALF:(j + 1) * HALF], lhsT=selector[:, m:m + 1].to_broadcast([P, P]),
                             rhs=src, start=True, stop=True)
            if j == 1:
                bias_tiles[m] = keep.tile([P, E], BF16, name="bias%d" % m)
                nc.scalar.copy(bias_tiles[m][:], bias_banks[m][:])

        def table(m, a):
            if (m, a) not in tables:
                tables[(m, a)] = keep.tile([P, E], F32, name="table%d_%d" % (m, a))
            return tables[(m, a)]

        def table_on_vector(m, a):
            nc.vector.tensor_scalar(table(m, a)[:], bias_tiles[m][:], cos_of(a), None, op0=ALU.mult)

        def half_table_on_scalar(m, a, j):
            cols = slice(j * HALF, (j + 1) * HALF)
            nc.scalar.activation(table(m, a)[:, cols], bias_tiles[m][:, cols], ACT.Copy, scale=cos_of(a))

        staged = {}
        codes = {}
        scales = {}

        def staged_words(unit):
            if unit not in staged:
                staged[unit] = stage.tile([P, 4 * HALF], BF16, name="staged", tag="staged", align_bytes=64)
            return staged[unit][:].bitcast(F32)

        def transpose_pass(key, g):
            bank = tpsum.tile([P, 2, 2, P], F32, name="turned", tag="turned")
            for j in range(2):
                words = raw[key][:, j, :].bitcast(F32)
                for u in range(2):
                    nc.tensor.transpose(bank[:, j, u, :], words[:, PASS_WORDS * g + u:PASS_WORDS * (g + 1):2], ident[:])
            return bank[:].rearrange("p j u r -> p j r u")

        def turn_w(m, c, g):
            bank = transpose_pass(("w%d" % m, c), g)
            dst = staged_words(("w", m, c // 2, g)).rearrange("p (j c r u) -> p j c r u", j=2, c=2, u=2)
            return dst[:, :, c % 2, :, :], bank

        def turn_x(q, g):
            bank = transpose_pass(("x", q), g)
            dst = staged_words(("x", q)).rearrange("p (g j r u) -> p g j r u", g=2, j=2, u=2)
            return dst[:, g, :, :, :], bank

        def turn_unit(unit):
            if unit[0] == "w":
                m, h, g = unit[1:]
                return [turn_w(m, 2 * h + c, g) for c in range(2)]
            return [turn_x(unit[1], g) for g in range(2)]

        def quantize(unit):
            name = "_".join(str(v) for v in unit)
            codes[unit] = keep.tile([P, HALF], U32, name="codes_" + name, align_bytes=64)
            scales[unit] = keep.tile([P, HALF], U8, name="scales_" + name, align_bytes=64)
            nc.vector.quantize_mx(out=codes[unit][:].bitcast(E5M2X4), scales=scales[unit][:], in_=staged[unit][:])

        banks = {}
        ys = {}
        tan_ys = {}

        def multiply(m, n, h):
            x_unit = ("x", n // 2)
            bank = mpsum.tile([P, HALF], F32, name="product", tag="product")
            banks[(m, n, h)] = bank
            for g in range(2):
                first = CHUNK * g + P * (n % 2)
                tokens = slice(first, first + P)
                w_unit = ("w", m, h, g)
                nc.tensor.matmul_mx(out=bank[:], lhsT=codes[x_unit][:, tokens].bitcast(E5M2X4),
                                    lhsT_scale=scales[x_unit][:, tokens],
                                    rhs=codes[w_unit][:].bitcast(E5M2X4), rhs_scale=scales[w_unit][:],
                                    start=(g == 0), stop=(g == 1))

        def angle_col(n):
            return 2 * X_CHUNKS[n // 2][1] + n % 2

        def add_bias(m, n, h):
            if h == 0:
                ys[(m, n)] = ypool.tile([P, E], F32, name="y", tag="y")
            y = ys[(m, n)]
            bank = banks[(m, n, h)]
            if m == MV:
                cols = slice(h * HALF, (h + 1) * HALF)
                nc.vector.tensor_tensor(y[:, cols].rearrange("p (r j) -> p r j", j=2),
                                        bank[:].rearrange("p (j r) -> p r j", j=2),
                                        bias_tiles[m][:, cols].rearrange("p (r j) -> p r j", j=2), op=ALU.add)
            else:
                a = angle_col(n)
                nc.vector.scalar_tensor_tensor(
                    y[:].rearrange("p (j h r) -> p j h r", j=2, h=2)[:, :, h, :],
                    bank[:].rearrange("p (j r) -> p j r", j=2),
                    cos_of(a),
                    tables[(m, a)][:].rearrange("p (j h r) -> p j h r", j=2, h=2)[:, :, h, :],
                    op0=ALU.mult, op1=ALU.add)

        def scale_by_tan(m, n):
            tan_y = tanpool.tile([P, E], F32, name="tan_y", tag="tan_y")
            tan_ys[(m, n)] = tan_y
            a = angle_col(n)
            y = ys[(m, n)]
            nc.scalar.activation(tan_y[:, 0:HALF], y[:, HALF:E], ACT.Copy, scale=ntan[:, a:a + 1])
            if m == MQ:
                nc.scalar.activation(tan_y[:, HALF:E], y[:, 0:HALF], ACT.Copy, scale=tan[:, a:a + 1])

        def rotate_shared(m, n):
            y = ys[(m, n)]
            a = angle_col(n)
            nc.vector.scalar_tensor_tensor(y[:, HALF:E], y[:, 0:HALF], tan[:, a:a + 1], y[:, HALF:E],
                                           op0=ALU.mult, op1=ALU.add)
            nc.gpsimd.tensor_tensor(y[:, 0:HALF], y[:, 0:HALF], tan_ys[(m, n)][:, 0:HALF], op=ALU.add)

        def rotate_whole(engine, m, n):
            y = ys[(m, n)]
            engine.tensor_tensor(y[:], y[:], tan_ys[(m, n)][:], op=ALU.add)

        def store(m, n):
            b, c = X_CHUNKS[n // 2]
            nc.sync.dma_start(out=outs[m][b, c, n % 2], in_=ys[(m, n)][:])

        nc.scalar.copy(*turn_w(MK, 0, 0))
        spread_bias(MK, 0)
        spread_bias(MK, 1)
        nc.vector.tensor_copy(*turn_w(MK, 0, 1))
        nc.scalar.copy(*turn_w(MK, 1, 0))
        spread_bias(MQ, 0)
        nc.vector.tensor_copy(*turn_w(MK, 1, 1))
        quantize(("w", MK, 0, 0))
        nc.scalar.copy(*turn_x(0, 0))
        spread_bias(MQ, 1)
        quantize(("w", MK, 0, 1))
        nc.vector.tensor_copy(*turn_x(0, 1))
        table_on_vector(MK, 0)
        quantize(("x", 0))
        nc.scalar.copy(*turn_w(MK, 2, 0))
        spread_bias(MV, 0)
        nc.scalar.copy(*turn_w(MK, 2, 1))
        table_on_vector(MK, 1)
        tangents()
        nc.scalar.copy(*turn_w(MK, 3, 0))
        spread_bias(MV, 1)
        nc.scalar.copy(*turn_w(MK, 3, 1))
        multiply(MK, 0, 0)
        multiply(MK, 1, 0)
        quantize(("w", MK, 1, 0))
        quantize(("w", MK, 1, 1))
        add_bias(MK, 0, 0)
        add_bias(MK, 1, 0)
        nc.scalar.copy(*turn_x(1, 0))
        nc.scalar.copy(*turn_x(1, 1))
        multiply(MK, 0, 1)
        multiply(MK, 1, 1)
        add_bias(MK, 0, 1)
        quantize(("x", 1))
        add_bias(MK, 1, 1)
        scale_by_tan(MK, 0)
        nc.scalar.copy(*turn_x(2, 0))
        nc.scalar.copy(*turn_x(2, 1))
        scale_by_tan(MK, 1)
        multiply(MK, 2, 0)
        multiply(MK, 2, 1)
        rotate_shared(MK, 0)

        wq = [("w", MQ, h, g) for h in range(2) for g in range(2)]
        wv = [("w", MV, h, g) for h in range(2) for g in range(2)]
        units = [[], [], [("x", 2)], wq[0:1], [("x", 3), wq[1]], wq[2:4], wv[0:1], wv[1:3], wv[3:4]]
        tiles = [(MK, n) for n in range(N_TILES)] + [(m, n) for n in range(N_TILES) for m in (MQ, MV)]
        last_q = (MQ, N_TILES - 1)
        half_tables = [(m, a, j) for m in (MK, MQ) for a in range(N_ANGLES) for j in range(2) if (m, a) not in tables]

        def units_at(s):
            return units[s] if s < len(units) else []

        def tile_at(s):
            return tiles[s] if s < len(tiles) else None

        def store_step(s):
            if tiles[s][0] == MV:
                return s + STORE_LAG_V
            return s + (STORE_LAG_Q if tiles[s][0] == MQ else STORE_LAG_K)

        for s in range(FIRST_STEP, max(store_step(r) for r in range(len(tiles))) + 1):
            now, last, before_last = tile_at(s), tile_at(s - 1), tile_at(s - 2)
            for dst, bank in [job for unit in units_at(s)[:1] for job in turn_unit(unit)]:
                nc.scalar.copy(dst, bank)
            if last:
                add_bias(*last, 0)
                add_bias(*last, 1)
            second_unit = [job for unit in units_at(s)[1:] for job in turn_unit(unit)]
            if last and last[0] != MV:
                scale_by_tan(*last)
            for dst, bank in second_unit:
                nc.scalar.copy(dst, bank)
            for unit in units_at(s - 1)[:-1]:
                quantize(unit)
            if before_last and before_last[0] == MK:
                rotate_shared(*before_last)
            for unit in units_at(s - 1)[-1:]:
                quantize(unit)
            for job in half_tables[:1 if s in SINGLE_TABLE_STEPS else 2]:
                half_table_on_scalar(*job)
                half_tables.remove(job)
            if now:
                multiply(*now, 0)
                multiply(*now, 1)
            if last and last[0] == MQ and last != last_q:
                rotate_whole(nc.gpsimd, *last)
            if before_last == last_q:
                rotate_whole(nc.vector, *last_q)
            for r in range(len(tiles)):
                if store_step(r) == s:
                    store(*tiles[r])
